import numpy as np
import ml_dtypes


def mxq(x, axis, fmt="e4m3"):
    dtype, down = {"e4m3": (ml_dtypes.float8_e4m3fn, 7), "e5m2": (ml_dtypes.float8_e5m2, 14)}[fmt]
    v = np.moveaxis(np.asarray(x, np.float32).astype(ml_dtypes.bfloat16).astype(np.float64), axis, -1)
    blocks = v.reshape(v.shape[:-1] + (-1, 32))
    amax = np.abs(blocks).max(-1, keepdims=True)
    byte = np.maximum(np.where(amax > 0, np.frexp(amax)[1] - 1 + 127, 0) - down, 1)
    scale = np.exp2(byte - 127.0)
    codes = (blocks / scale).astype(np.float32).astype(dtype).astype(np.float64)
    return np.moveaxis((codes * scale).reshape(v.shape), -1, axis)


WIDE = False


def mx_kscale(k):
    if not WIDE:
        return np.ones(k)
    levels = np.array([10, -10, 5, -5, 0])
    a = np.random.permutation(np.resize(levels, k // 512 * 4)).reshape(k // 512, 4)
    idx = np.arange(k)
    return np.exp2(a[idx // 512, idx % 128 // 32])


BF16 = ml_dtypes.bfloat16


def bf(x):
    return np.asarray(x, np.float32).astype(BF16)


def f64(x):
    return np.asarray(x).astype(np.float64)


E2M1 = np.array([0.0, 0.5, 1.0, 1.5, 2.0, 3.0, 4.0, 6.0, -0.0, -0.5, -1.0, -1.5, -2.0, -3.0, -4.0, -6.0])


def pack_weight(w, fmt):
    k, n = w.shape
    w = f64(bf(w)).reshape(k // 32, 32, n)
    amax = np.abs(w).max(1)
    if fmt == "e4m3":
        byte = np.frexp(amax)[1] - 1 + 127 - 7
    else:
        mant, ex = np.frexp(amax / 6.0)
        byte = np.where(mant > 0.5, ex, ex - 1) + 127
    byte = np.clip(np.where(amax > 0, byte, 1), 1, 254)
    scaled = (w * np.exp2(127.0 - byte)[:, None, :]).reshape(k, n).astype(np.float32)
    by_word = np.ascontiguousarray(scaled.reshape(k // 512, 128, 4, n).transpose(0, 1, 3, 2))
    if fmt == "e4m3":
        words = by_word.astype(ml_dtypes.float8_e4m3fn).view(np.uint8)
    else:
        c = by_word.astype(ml_dtypes.float4_e2m1fn).view(np.uint8) & 0xF
        words = c[..., 0::2] | (c[..., 1::2] << 4)
    return np.ascontiguousarray(words), np.ascontiguousarray(byte.astype(np.uint8).reshape(k // 512, 16, n))


def unpack_weight(words, scales, fmt):
    g, p, n, _ = words.shape
    if fmt == "e4m3":
        vals = np.ascontiguousarray(words).view(ml_dtypes.float8_e4m3fn).astype(np.float64)
    else:
        nib = np.empty((g, p, n, 4), np.uint8)
        nib[..., 0::2] = words & 0xF
        nib[..., 1::2] = words >> 4
        vals = E2M1[nib]
    vals = vals * np.repeat(np.exp2(scales.astype(np.float64) - 127.0), 8, axis=1)[..., None]
    return vals.transpose(0, 1, 3, 2).reshape(g * 512, n)

def pack4(w):
    words, scales = pack_weight(w, "e2m1")
    return words.reshape(words.shape[0], 128, -1), scales


def unpack4(words, scales):
    return unpack_weight(words.reshape(words.shape[0], 128, -1, 2), scales, "e2m1")


N, P, D, E, F = 5120, 3, 512, 512, 128
BN_EPS = 1e-5


def setup_inputs():
    t = mx_kscale(E)
    h = 1.2 * np.random.standard_normal((N, P, E)) + 0.6 * np.random.standard_normal((1, P, E))
    w1b_words, w1b_scales = pack4(np.random.standard_normal((E, F)) / np.sqrt(E) / t[:, None])
    w2b_words, w2b_scales = pack4(np.random.standard_normal((E, F)) / np.sqrt(E) / t[:, None])
    return {"h_sage": bf(h * t),
            "w1b_words": w1b_words,
            "w1b_scales": w1b_scales,
            "w2b_words": w2b_words,
            "w2b_scales": w2b_scales,
            "gamma": bf(1.0 + 0.2 * np.random.standard_normal(F)),
            "beta": bf(0.3 * np.random.standard_normal(F))}


def reference(h_sage, w1b_words, w1b_scales, w2b_words, w2b_scales, gamma, beta):
    h = f64(h_sage)
    neigh = (h.sum(axis=1, keepdims=True) - h) * 0.5
    out = (mxq(h[:, 0, :], 1, "e4m3") @ unpack4(w2b_words, w2b_scales)) + (mxq(neigh[:, 0, :], 1, "e4m3") @ unpack4(w1b_words, w1b_scales))
    mean = out.mean(axis=0)
    var = out.var(axis=0)
    out = (out - mean) / np.sqrt(var + BN_EPS) * f64(gamma) + f64(beta)
    return 1.0 / (1.0 + np.exp(-out))

@@ -1,0 +1,203 @@
+from contextlib import ExitStack
+
+import concourse.mybir as mybir
+from concourse.masks import make_identity
+
+F32 = mybir.dt.float32
+BF16 = mybir.dt.bfloat16
+I32 = mybir.dt.int32
+U32 = mybir.dt.uint32
+U8 = mybir.dt.uint8
+FP8X4 = mybir.dt.float8_e4m3fn_x4
+FP4X4 = mybir.dt.float4_e2m1fn_x4
+ALU = mybir.AluOpType
+ACT = mybir.ActivationFunctionType
+
+P = 128
+ITEMS = 5120
+HOPS = 3
+FEATURES = 512
+OUT_COLS = 128
+BN_EPS = 1e-5
+
+PACK = 4
+WORDS = FEATURES // 2
+TILES = ITEMS // P
+CHUNK_TILES = 4
+CHUNK_ITEMS = CHUNK_TILES * P
+CHUNKS = TILES // CHUNK_TILES
+BN_STATS_DIM = 6
+
+SELF = 0
+NEIGH = 1
+
+FLOPS = 2 * 2 * ITEMS * FEATURES * OUT_COLS
+
+
+def tile_dogtaitujuanji_pb_t_kernel(
+    tc, h_sage, w1b_words, w1b_scales, w2b_words, w2b_scales, gamma, beta, out
+):
+    nc = tc.nc
+    h_by_partition = h_sage.rearrange("(p t) q k -> p t q k", t=TILES)
+    out_by_partition = out.rearrange("(p t) f -> p t f", t=TILES)
+
+    with ExitStack() as stack:
+        keep = stack.enter_context(tc.tile_pool(name="keep", bufs=1))
+        h_pool = stack.enter_context(tc.tile_pool(name="h", bufs=CHUNKS))
+        mean_pool = stack.enter_context(tc.tile_pool(name="mean", bufs=2))
+        mx_pool = stack.enter_context(tc.tile_pool(name="mx", bufs=3))
+        out_pool = stack.enter_context(tc.tile_pool(name="out", bufs=4))
+        bank_pool = stack.enter_context(tc.psum_pool(name="bank", bufs=6))
+        y_pool = stack.enter_context(tc.psum_pool(name="y", bufs=2))
+        stack.enter_context(tc.manual_schedule())
+
+        gb_rows = keep.tile([P, P], BF16)
+        nc.vector.memset(gb_rows[:], 0.0)
+        nc.gpsimd.dma_start(out=gb_rows[0:1, :], in_=gamma.rearrange("(o f) -> o f", o=1))
+        nc.gpsimd.dma_start(out=gb_rows[1:2, :], in_=beta.rearrange("(o f) -> o f", o=1))
+
+        w_words = keep.tile([P, 2, 2 * OUT_COLS], U8, align_bytes=64)
+        w_planes = keep.tile([P, 2, OUT_COLS], U8, align_bytes=64)
+        nc.vector.memset(w_planes[:].bitcast(I32), 0)
+        for operand, words, scale_rows in ((SELF, w2b_words, w2b_scales), (NEIGH, w1b_words, w1b_scales)):
+            nc.sync.dma_start(out=w_words[:, operand, :].bitcast(I32), in_=words[0, :, :].bitcast(I32))
+            for r in range(4):
+                nc.sync.dma_start(
+                    out=w_planes[r:P:32, operand, :].bitcast(I32),
+                    in_=scale_rows[0, r:16:4, :].bitcast(I32),
+                )
+
+        h_chunks = []
+        for c in range(CHUNKS):
+            h_chunk = h_pool.tile([P, CHUNK_TILES, HOPS, FEATURES], BF16)
+            nc.sync.dma_start(
+                out=h_chunk[:], in_=h_by_partition[:, c * CHUNK_TILES : (c + 1) * CHUNK_TILES, :, :]
+            )
+            h_chunks.append(h_chunk)
+
+        ident = keep.tile([P, P], F32)
+        make_identity(nc, ident[:])
+        ident_bf = keep.tile([P, P], BF16)
+        nc.vector.tensor_copy(out=ident_bf[:], in_=ident[:])
+        minus_half = keep.tile([P, 1], F32)
+        nc.vector.memset(minus_half[:], -0.5)
+
+        table_in = keep.tile([P, 1], F32)
+        table_out = keep.tile([P, 1], F32)
+        nc.vector.memset(table_in[:], 0.0)
+        nc.scalar.activation(out=table_out[:], in_=table_in[:], func=ACT.Sigmoid)
+
+        gb_bank = bank_pool.tile([P, P], BF16, tag="bank")
+        nc.tensor.transpose(gb_bank[:], gb_rows[:], ident_bf[:])
+        gamma_beta = keep.tile([P, 2], F32)
+        nc.vector.tensor_copy(out=gamma_beta[:], in_=gb_bank[:, 0:2])
+        gamma_col = gamma_beta[:, 0:1]
+        beta_col = gamma_beta[:, 1:2]
+        minus_gamma = keep.tile([P, 1], F32)
+        nc.vector.tensor_scalar(out=minus_gamma[:], in0=gamma_col, scalar1=-1.0, scalar2=None, op0=ALU.mult)
+
+        y_all = keep.tile([P, ITEMS], F32)
+        stats = keep.tile([P, CHUNKS, BN_STATS_DIM], F32)
+
+        def average_neighbours(c):
+            hop_sum = mean_pool.tile([P, CHUNK_TILES, FEATURES], BF16)
+            nc.vector.tensor_tensor(
+                out=hop_sum[:], in0=h_chunks[c][:, :, 1, :], in1=h_chunks[c][:, :, 2, :], op=ALU.add
+            )
+            neigh = mean_pool.tile([P, CHUNK_TILES, FEATURES], BF16)
+            nc.vector.tensor_scalar(out=neigh[:], in0=hop_sum[:], scalar1=0.5, scalar2=None, op0=ALU.mult)
+            return neigh
+
+        def features_to_partitions(item_rows, grouped_words):
+            for pair in range(CHUNK_TILES // 2):
+                bank = bank_pool.tile([P, 2, 2 * P], F32, tag="bank")
+                for a in range(2):
+                    row_words = item_rows(2 * pair + a).bitcast(F32)
+                    for u in range(2):
+                        nc.tensor.transpose(bank[:, u, a * P : (a + 1) * P], row_words[:, u:WORDS:2], ident[:])
+                nc.scalar.copy(
+                    out=grouped_words[:, 2 * pair * P : 2 * (pair + 1) * P, :],
+                    in_=bank[:].rearrange("p u i -> p i u"),
+                )
+
+        def regroup(c, neigh):
+            grouped = mx_pool.tile([P, 2, CHUNK_ITEMS * PACK], BF16, align_bytes=64)
+            features_to_partitions(
+                lambda a: h_chunks[c][:, a, 0, :],
+                grouped[:, SELF, :].bitcast(F32).rearrange("p (i u) -> p i u", u=2),
+            )
+            features_to_partitions(
+                lambda a: neigh[:, a, :],
+                grouped[:, NEIGH, :].bitcast(F32).rearrange("p (i u) -> p i u", u=2),
+            )
+            return grouped
+
+        def quantise(grouped):
+            codes = mx_pool.tile([P, 2, CHUNK_ITEMS], U32, align_bytes=64)
+            scales = mx_pool.tile([P, 2, CHUNK_ITEMS], U8, align_bytes=64)
+            nc.vector.quantize_mx(
+                out=codes[:].rearrange("p o i -> p (o i)").bitcast(FP8X4),
+                scales=scales[:].rearrange("p o i -> p (o i)"),
+                in_=grouped[:].rearrange("p o e -> p (o e)"),
+            )
+            return codes, scales
+
+        def multiply(c, codes, scales):
+            y_bank = y_pool.tile([P, CHUNK_ITEMS], F32)
+            for operand in (SELF, NEIGH):
+                nc.tensor.matmul_mx(
+                    out=y_bank[:],
+                    lhsT=w_words[:, operand, :].bitcast(FP4X4),
+                    lhsT_scale=w_planes[:, operand, :],
+                    rhs=codes[:, operand, :].bitcast(FP8X4),
+                    rhs_scale=scales[:, operand, :],
+                    start=(operand == SELF),
+                    stop=(operand == NEIGH),
+                )
+            nc.scalar.copy(out=y_all[:, c * CHUNK_ITEMS : (c + 1) * CHUNK_ITEMS], in_=y_bank[:])
+
+        def gather_statistics(c):
+            nc.vector.bn_stats(out=stats[:, c, :], in_=y_all[:, c * CHUNK_ITEMS : (c + 1) * CHUNK_ITEMS])
+
+        grouped_of = {}
+        for c in range(CHUNKS + 2):
+            if c < CHUNKS:
+                grouped_of[c] = regroup(c, average_neighbours(c))
+            if 1 <= c <= CHUNKS:
+                codes, scales = quantise(grouped_of[c - 1])
+                multiply(c - 1, codes, scales)
+            if c >= 2:
+                gather_statistics(c - 2)
+
+        mean_var = keep.tile([P, 2], F32)
+        nc.vector.bn_aggr(out=mean_var[:], in_=stats[:].rearrange("p c s -> p (c s)"))
+        var_eps = keep.tile([P, 1], F32)
+        nc.vector.tensor_scalar(out=var_eps[:], in0=mean_var[:, 1:2], scalar1=BN_EPS, scalar2=None, op0=ALU.add)
+        inv_std = keep.tile([P, 1], F32)
+        nc.gpsimd.tensor_tensor(out=inv_std[:], in0=var_eps[:], in1=minus_half[:], op=ALU.pow)
+        minus_mean_gamma = keep.tile([P, 1], F32)
+        nc.vector.tensor_tensor(out=minus_mean_gamma[:], in0=mean_var[:, 0:1], in1=minus_gamma[:], op=ALU.mult)
+        slope = keep.tile([P, 1], F32)
+        nc.vector.tensor_tensor(out=slope[:], in0=gamma_col, in1=inv_std[:], op=ALU.mult)
+        shift = keep.tile([P, 1], F32)
+        nc.vector.scalar_tensor_tensor(
+            out=shift[:], in0=minus_mean_gamma[:], scalar=inv_std[:, 0:1], in1=beta_col, op0=ALU.mult, op1=ALU.add
+        )
+
+        for c in range(CHUNKS):
+            sig = out_pool.tile([P, CHUNK_ITEMS], F32)
+            nc.scalar.activation(
+                out=sig[:],
+                in_=y_all[:, c * CHUNK_ITEMS : (c + 1) * CHUNK_ITEMS],
+                func=ACT.Sigmoid,
+                bias=shift[:, 0:1],
+                scale=slope[:, 0:1],
+            )
+            out_bank = bank_pool.tile([P, CHUNK_TILES, OUT_COLS], F32, tag="bank")
+            for a in range(CHUNK_TILES):
+                nc.tensor.transpose(out_bank[:, a, :], sig[:, a * P : (a + 1) * P], ident[:])
+            out_rows = out_pool.tile([P, CHUNK_TILES, OUT_COLS], F32)
+            nc.vector.tensor_copy(out=out_rows[:], in_=out_bank[:])
+            nc.sync.dma_start(
+                out=out_by_partition[:, c * CHUNK_TILES : (c + 1) * CHUNK_TILES, :], in_=out_rows[:]
+            )

@@ -27,6 +27,8 @@ CHUNK_TILES = 4
 CHUNK_ITEMS = CHUNK_TILES * P
 CHUNKS = TILES // CHUNK_TILES
 BN_STATS_DIM = 6
+Y_BANKS = 2
+PREFETCH = 6
 
 SELF = 0
 NEIGH = 1
@@ -48,13 +50,24 @@ def tile_dogtaitujuanji_pb_t_kernel(
         mx_pool = stack.enter_context(tc.tile_pool(name="mx", bufs=3))
         out_pool = stack.enter_context(tc.tile_pool(name="out", bufs=4))
         bank_pool = stack.enter_context(tc.psum_pool(name="bank", bufs=6))
-        y_pool = stack.enter_context(tc.psum_pool(name="y", bufs=2))
+        y_pool = stack.enter_context(tc.psum_pool(name="y", bufs=Y_BANKS))
         stack.enter_context(tc.manual_schedule())
+
+        h_chunks = {}
+
+        def load(c):
+            h_chunk = h_pool.tile([P, CHUNK_TILES, HOPS, FEATURES], BF16)
+            nc.scalar.dma_start(
+                out=h_chunk[:], in_=h_by_partition[:, c * CHUNK_TILES : (c + 1) * CHUNK_TILES, :, :]
+            )
+            h_chunks[c] = h_chunk
 
         gb_rows = keep.tile([P, P], BF16)
         nc.vector.memset(gb_rows[:], 0.0)
-        nc.gpsimd.dma_start(out=gb_rows[0:1, :], in_=gamma.rearrange("(o f) -> o f", o=1))
-        nc.gpsimd.dma_start(out=gb_rows[1:2, :], in_=beta.rearrange("(o f) -> o f", o=1))
+        nc.sync.dma_start(out=gb_rows[0:1, :], in_=gamma.rearrange("(o f) -> o f", o=1))
+        nc.sync.dma_start(out=gb_rows[1:2, :], in_=beta.rearrange("(o f) -> o f", o=1))
+
+        load(0)
 
         w_words = keep.tile([P, 2, 2 * OUT_COLS], U8, align_bytes=64)
         w_planes = keep.tile([P, 2, OUT_COLS], U8, align_bytes=64)
@@ -67,13 +80,13 @@ def tile_dogtaitujuanji_pb_t_kernel(
                     in_=scale_rows[0, r:16:4, :].bitcast(I32),
                 )
 
-        h_chunks = []
-        for c in range(CHUNKS):
-            h_chunk = h_pool.tile([P, CHUNK_TILES, HOPS, FEATURES], BF16)
-            nc.sync.dma_start(
-                out=h_chunk[:], in_=h_by_partition[:, c * CHUNK_TILES : (c + 1) * CHUNK_TILES, :, :]
-            )
-            h_chunks.append(h_chunk)
+        table_in = keep.tile([P, 1], F32)
+        table_out = keep.tile([P, 1], F32)
+        nc.vector.memset(table_in[:], 0.0)
+        nc.scalar.activation(out=table_out[:], in_=table_in[:], func=ACT.Sigmoid)
+
+        for c in range(1, PREFETCH):
+            load(c)
 
         ident = keep.tile([P, P], F32)
         make_identity(nc, ident[:])
@@ -81,11 +94,6 @@ def tile_dogtaitujuanji_pb_t_kernel(
         nc.vector.tensor_copy(out=ident_bf[:], in_=ident[:])
         minus_half = keep.tile([P, 1], F32)
         nc.vector.memset(minus_half[:], -0.5)
-
-        table_in = keep.tile([P, 1], F32)
-        table_out = keep.tile([P, 1], F32)
-        nc.vector.memset(table_in[:], 0.0)
-        nc.scalar.activation(out=table_out[:], in_=table_in[:], func=ACT.Sigmoid)
 
         gb_bank = bank_pool.tile([P, P], BF16, tag="bank")
         nc.tensor.transpose(gb_bank[:], gb_rows[:], ident_bf[:])
@@ -96,8 +104,13 @@ def tile_dogtaitujuanji_pb_t_kernel(
         minus_gamma = keep.tile([P, 1], F32)
         nc.vector.tensor_scalar(out=minus_gamma[:], in0=gamma_col, scalar1=-1.0, scalar2=None, op0=ALU.mult)
 
-        y_all = keep.tile([P, ITEMS], F32)
+        y_sbuf = keep.tile([P, (CHUNKS - Y_BANKS) * CHUNK_ITEMS], F32)
+        y_of = {}
         stats = keep.tile([P, CHUNKS, BN_STATS_DIM], F32)
+
+        grouped_of = {}
+        codes_of = {}
+        scales_of = {}
 
         def average_neighbours(c):
             hop_sum = mean_pool.tile([P, CHUNK_TILES, FEATURES], BF16)
@@ -108,7 +121,8 @@ def tile_dogtaitujuanji_pb_t_kernel(
             nc.vector.tensor_scalar(out=neigh[:], in0=hop_sum[:], scalar1=0.5, scalar2=None, op0=ALU.mult)
             return neigh
 
-        def features_to_partitions(item_rows, grouped_words):
+        def features_to_partitions(item_rows, grouped):
+            grouped_words = grouped.bitcast(F32).rearrange("p (i u) -> p i u", u=2)
             for pair in range(CHUNK_TILES // 2):
                 bank = bank_pool.tile([P, 2, 2 * P], F32, tag="bank")
                 for a in range(2):
@@ -122,52 +136,52 @@ def tile_dogtaitujuanji_pb_t_kernel(
 
         def regroup(c, neigh):
             grouped = mx_pool.tile([P, 2, CHUNK_ITEMS * PACK], BF16, align_bytes=64)
-            features_to_partitions(
-                lambda a: h_chunks[c][:, a, 0, :],
-                grouped[:, SELF, :].bitcast(F32).rearrange("p (i u) -> p i u", u=2),
-            )
-            features_to_partitions(
-                lambda a: neigh[:, a, :],
-                grouped[:, NEIGH, :].bitcast(F32).rearrange("p (i u) -> p i u", u=2),
-            )
-            return grouped
+            features_to_partitions(lambda a: h_chunks[c][:, a, 0, :], grouped[:, SELF, :])
+            features_to_partitions(lambda a: neigh[:, a, :], grouped[:, NEIGH, :])
+            grouped_of[c] = grouped
+            codes_of[c] = mx_pool.tile([P, 2, CHUNK_ITEMS], U32, align_bytes=64, name="codes")
+            scales_of[c] = mx_pool.tile([P, 2, CHUNK_ITEMS], U8, align_bytes=64, name="scales")
 
-        def quantise(grouped):
-            codes = mx_pool.tile([P, 2, CHUNK_ITEMS], U32, align_bytes=64)
-            scales = mx_pool.tile([P, 2, CHUNK_ITEMS], U8, align_bytes=64)
+        def quantise(c, operand):
             nc.vector.quantize_mx(
-                out=codes[:].rearrange("p o i -> p (o i)").bitcast(FP8X4),
-                scales=scales[:].rearrange("p o i -> p (o i)"),
-                in_=grouped[:].rearrange("p o e -> p (o e)"),
+                out=codes_of[c][:, operand, :].bitcast(FP8X4),
+                scales=scales_of[c][:, operand, :],
+                in_=grouped_of[c][:, operand, :],
             )
-            return codes, scales
 
-        def multiply(c, codes, scales):
+        def multiply(c):
             y_bank = y_pool.tile([P, CHUNK_ITEMS], F32)
             for operand in (SELF, NEIGH):
                 nc.tensor.matmul_mx(
                     out=y_bank[:],
                     lhsT=w_words[:, operand, :].bitcast(FP4X4),
                     lhsT_scale=w_planes[:, operand, :],
-                    rhs=codes[:, operand, :].bitcast(FP8X4),
-                    rhs_scale=scales[:, operand, :],
+                    rhs=codes_of[c][:, operand, :].bitcast(FP8X4),
+                    rhs_scale=scales_of[c][:, operand, :],
                     start=(operand == SELF),
                     stop=(operand == NEIGH),
                 )
-            nc.scalar.copy(out=y_all[:, c * CHUNK_ITEMS : (c + 1) * CHUNK_ITEMS], in_=y_bank[:])
+            if c < CHUNKS - Y_BANKS:
+                y_of[c] = y_sbuf[:, c * CHUNK_ITEMS : (c + 1) * CHUNK_ITEMS]
+                nc.scalar.copy(out=y_of[c], in_=y_bank[:])
+            else:
+                y_of[c] = y_bank[:]
 
         def gather_statistics(c):
-            nc.vector.bn_stats(out=stats[:, c, :], in_=y_all[:, c * CHUNK_ITEMS : (c + 1) * CHUNK_ITEMS])
+            nc.vector.bn_stats(out=stats[:, c, :], in_=y_of[c])
 
-        grouped_of = {}
         for c in range(CHUNKS + 2):
             if c < CHUNKS:
-                grouped_of[c] = regroup(c, average_neighbours(c))
+                regroup(c, average_neighbours(c))
             if 1 <= c <= CHUNKS:
-                codes, scales = quantise(grouped_of[c - 1])
-                multiply(c - 1, codes, scales)
+                quantise(c - 1, NEIGH)
+                multiply(c - 1)
             if c >= 2:
                 gather_statistics(c - 2)
+            if c < CHUNKS:
+                quantise(c, SELF)
+            if c + PREFETCH < CHUNKS:
+                load(c + PREFETCH)
 
         mean_var = keep.tile([P, 2], F32)
         nc.vector.bn_aggr(out=mean_var[:], in_=stats[:].rearrange("p c s -> p (c s)"))
@@ -186,13 +200,7 @@ def tile_dogtaitujuanji_pb_t_kernel(
 
         for c in range(CHUNKS):
             sig = out_pool.tile([P, CHUNK_ITEMS], F32)
-            nc.scalar.activation(
-                out=sig[:],
-                in_=y_all[:, c * CHUNK_ITEMS : (c + 1) * CHUNK_ITEMS],
-                func=ACT.Sigmoid,
-                bias=shift[:, 0:1],
-                scale=slope[:, 0:1],
-            )
+            nc.scalar.activation(out=sig[:], in_=y_of[c], func=ACT.Sigmoid, bias=shift[:, 0:1], scale=slope[:, 0:1])
             out_bank = bank_pool.tile([P, CHUNK_TILES, OUT_COLS], F32, tag="bank")
             for a in range(CHUNK_TILES):
                 nc.tensor.transpose(out_bank[:, a, :], sig[:, a * P : (a + 1) * P], ident[:])

@@ -28,7 +28,6 @@ CHUNK_ITEMS = CHUNK_TILES * P
 CHUNKS = TILES // CHUNK_TILES
 BN_STATS_DIM = 6
 Y_BANKS = 2
-PREFETCH = 6
 
 SELF = 0
 NEIGH = 1
@@ -57,36 +56,38 @@ def tile_dogtaitujuanji_pb_t_kernel(
 
         def load(c):
             h_chunk = h_pool.tile([P, CHUNK_TILES, HOPS, FEATURES], BF16)
-            nc.scalar.dma_start(
+            nc.sync.dma_start(
                 out=h_chunk[:], in_=h_by_partition[:, c * CHUNK_TILES : (c + 1) * CHUNK_TILES, :, :]
             )
             h_chunks[c] = h_chunk
 
-        gb_rows = keep.tile([P, P], BF16)
-        nc.vector.memset(gb_rows[:], 0.0)
-        nc.sync.dma_start(out=gb_rows[0:1, :], in_=gamma.rearrange("(o f) -> o f", o=1))
-        nc.sync.dma_start(out=gb_rows[1:2, :], in_=beta.rearrange("(o f) -> o f", o=1))
-
-        load(0)
-
         w_words = keep.tile([P, 2, 2 * OUT_COLS], U8, align_bytes=64)
         w_planes = keep.tile([P, 2, OUT_COLS], U8, align_bytes=64)
         nc.vector.memset(w_planes[:].bitcast(I32), 0)
-        for operand, words, scale_rows in ((SELF, w2b_words, w2b_scales), (NEIGH, w1b_words, w1b_scales)):
+
+        def load_words(operand, words):
             nc.sync.dma_start(out=w_words[:, operand, :].bitcast(I32), in_=words[0, :, :].bitcast(I32))
+
+        def load_scales(operand, scale_rows):
             for r in range(4):
                 nc.sync.dma_start(
                     out=w_planes[r:P:32, operand, :].bitcast(I32),
                     in_=scale_rows[0, r:16:4, :].bitcast(I32),
                 )
 
+        load(0)
+        load_words(SELF, w2b_words)
+        load_scales(SELF, w2b_scales)
+        load_words(NEIGH, w1b_words)
+        load(1)
+        load_scales(NEIGH, w1b_scales)
+        for c in range(2, CHUNKS):
+            load(c)
+
         table_in = keep.tile([P, 1], F32)
         table_out = keep.tile([P, 1], F32)
         nc.vector.memset(table_in[:], 0.0)
         nc.scalar.activation(out=table_out[:], in_=table_in[:], func=ACT.Sigmoid)
-
-        for c in range(1, PREFETCH):
-            load(c)
 
         ident = keep.tile([P, P], F32)
         make_identity(nc, ident[:])
@@ -95,30 +96,30 @@ def tile_dogtaitujuanji_pb_t_kernel(
         minus_half = keep.tile([P, 1], F32)
         nc.vector.memset(minus_half[:], -0.5)
 
-        gb_bank = bank_pool.tile([P, P], BF16, tag="bank")
-        nc.tensor.transpose(gb_bank[:], gb_rows[:], ident_bf[:])
-        gamma_beta = keep.tile([P, 2], F32)
-        nc.vector.tensor_copy(out=gamma_beta[:], in_=gb_bank[:, 0:2])
-        gamma_col = gamma_beta[:, 0:1]
-        beta_col = gamma_beta[:, 1:2]
-        minus_gamma = keep.tile([P, 1], F32)
-        nc.vector.tensor_scalar(out=minus_gamma[:], in0=gamma_col, scalar1=-1.0, scalar2=None, op0=ALU.mult)
+        gb_rows = keep.tile([P, P], BF16)
+        nc.vector.memset(gb_rows[:], 0.0)
+        nc.gpsimd.dma_start(out=gb_rows[0:1, :], in_=gamma.rearrange("(o f) -> o f", o=1))
+        nc.gpsimd.dma_start(out=gb_rows[1:2, :], in_=beta.rearrange("(o f) -> o f", o=1))
 
         y_sbuf = keep.tile([P, (CHUNKS - Y_BANKS) * CHUNK_ITEMS], F32)
         y_of = {}
         stats = keep.tile([P, CHUNKS, BN_STATS_DIM], F32)
 
+        hop_sum_of = {}
         grouped_of = {}
         codes_of = {}
         scales_of = {}
 
-        def average_neighbours(c):
+        def add_hops(c):
             hop_sum = mean_pool.tile([P, CHUNK_TILES, FEATURES], BF16)
             nc.vector.tensor_tensor(
                 out=hop_sum[:], in0=h_chunks[c][:, :, 1, :], in1=h_chunks[c][:, :, 2, :], op=ALU.add
             )
+            hop_sum_of[c] = hop_sum
+
+        def halve(c):
             neigh = mean_pool.tile([P, CHUNK_TILES, FEATURES], BF16)
-            nc.vector.tensor_scalar(out=neigh[:], in0=hop_sum[:], scalar1=0.5, scalar2=None, op0=ALU.mult)
+            nc.vector.tensor_scalar(out=neigh[:], in0=hop_sum_of[c][:], scalar1=0.5, scalar2=None, op0=ALU.mult)
             return neigh
 
         def features_to_partitions(item_rows, grouped):
@@ -170,18 +171,30 @@ def tile_dogtaitujuanji_pb_t_kernel(
         def gather_statistics(c):
             nc.vector.bn_stats(out=stats[:, c, :], in_=y_of[c])
 
-        for c in range(CHUNKS + 2):
+        add_hops(0)
+        for c in range(CHUNKS + 1):
             if c < CHUNKS:
-                regroup(c, average_neighbours(c))
-            if 1 <= c <= CHUNKS:
+                regroup(c, halve(c))
+            if c >= 1:
                 quantise(c - 1, NEIGH)
                 multiply(c - 1)
             if c >= 2:
                 gather_statistics(c - 2)
+            if c + 1 < CHUNKS:
+                add_hops(c + 1)
             if c < CHUNKS:
                 quantise(c, SELF)
-            if c + PREFETCH < CHUNKS:
-                load(c + PREFETCH)
+
+        gb_bank = bank_pool.tile([P, P], BF16, tag="bank")
+        nc.tensor.transpose(gb_bank[:], gb_rows[:], ident_bf[:])
+        gamma_beta = keep.tile([P, 2], F32)
+        nc.vector.tensor_copy(out=gamma_beta[:], in_=gb_bank[:, 0:2])
+        gamma_col = gamma_beta[:, 0:1]
+        beta_col = gamma_beta[:, 1:2]
+        minus_gamma = keep.tile([P, 1], F32)
+        nc.vector.tensor_scalar(out=minus_gamma[:], in0=gamma_col, scalar1=-1.0, scalar2=None, op0=ALU.mult)
+
+        gather_statistics(CHUNKS - 1)
 
         mean_var = keep.tile([P, 2], F32)
         nc.vector.bn_aggr(out=mean_var[:], in_=stats[:].rearrange("p c s -> p (c s)"))
@@ -198,14 +211,13 @@ def tile_dogtaitujuanji_pb_t_kernel(
             out=shift[:], in0=minus_mean_gamma[:], scalar=inv_std[:, 0:1], in1=beta_col, op0=ALU.mult, op1=ALU.add
         )
 
+        out_rows = keep.tile([P, TILES, OUT_COLS], F32)
         for c in range(CHUNKS):
             sig = out_pool.tile([P, CHUNK_ITEMS], F32)
             nc.scalar.activation(out=sig[:], in_=y_of[c], func=ACT.Sigmoid, bias=shift[:, 0:1], scale=slope[:, 0:1])
             out_bank = bank_pool.tile([P, CHUNK_TILES, OUT_COLS], F32, tag="bank")
             for a in range(CHUNK_TILES):
                 nc.tensor.transpose(out_bank[:, a, :], sig[:, a * P : (a + 1) * P], ident[:])
-            out_rows = out_pool.tile([P, CHUNK_TILES, OUT_COLS], F32)
-            nc.vector.tensor_copy(out=out_rows[:], in_=out_bank[:])
-            nc.sync.dma_start(
-                out=out_by_partition[:, c * CHUNK_TILES : (c + 1) * CHUNK_TILES, :], in_=out_rows[:]
-            )
+            tiles = slice(c * CHUNK_TILES, (c + 1) * CHUNK_TILES)
+            nc.vector.tensor_copy(out=out_rows[:, tiles, :], in_=out_bank[:])
+            nc.sync.dma_start(out=out_by_partition[:, tiles, :], in_=out_rows[:, tiles, :])

@@ -50,7 +50,6 @@ def tile_dogtaitujuanji_pb_t_kernel(
         out_pool = stack.enter_context(tc.tile_pool(name="out", bufs=4))
         bank_pool = stack.enter_context(tc.psum_pool(name="bank", bufs=6))
         y_pool = stack.enter_context(tc.psum_pool(name="y", bufs=Y_BANKS))
-        stack.enter_context(tc.manual_schedule())
 
         h_chunks = {}
 

@@ -21,13 +21,20 @@ OUT_COLS = 128
 BN_EPS = 1e-5
 
 PACK = 4
-WORDS = FEATURES // 2
-TILES = ITEMS // P
-CHUNK_TILES = 4
-CHUNK_ITEMS = CHUNK_TILES * P
-CHUNKS = TILES // CHUNK_TILES
+PAIRS = FEATURES // 2
+QUADRANT = 32
+BLOCKS = FEATURES // 32
+QUADRANT_BLOCKS = QUADRANT // 8
+
+LAYERS = ITEMS // P
+CHUNK_LAYERS = 4
+CHUNK_ITEMS = CHUNK_LAYERS * P
+CHUNKS = LAYERS // CHUNK_LAYERS
 BN_STATS_DIM = 6
+
+PSUM_BANKS = 8
 Y_BANKS = 2
+TRANSPOSE_BANKS = PSUM_BANKS - Y_BANKS
 
 SELF = 0
 NEIGH = 1
@@ -39,8 +46,8 @@ def tile_dogtaitujuanji_pb_t_kernel(
     tc, h_sage, w1b_words, w1b_scales, w2b_words, w2b_scales, gamma, beta, out
 ):
     nc = tc.nc
-    h_by_partition = h_sage.rearrange("(p t) q k -> p t q k", t=TILES)
-    out_by_partition = out.rearrange("(p t) f -> p t f", t=TILES)
+    h_by_partition = h_sage.rearrange("(p t) q k -> p t q k", t=LAYERS)
+    out_by_partition = out.rearrange("(p t) f -> p t f", t=LAYERS)
 
     with ExitStack() as stack:
         keep = stack.enter_context(tc.tile_pool(name="keep", bufs=1))
@@ -48,15 +55,16 @@ def tile_dogtaitujuanji_pb_t_kernel(
         mean_pool = stack.enter_context(tc.tile_pool(name="mean", bufs=2))
         mx_pool = stack.enter_context(tc.tile_pool(name="mx", bufs=3))
         out_pool = stack.enter_context(tc.tile_pool(name="out", bufs=4))
-        bank_pool = stack.enter_context(tc.psum_pool(name="bank", bufs=6))
+        bank_pool = stack.enter_context(tc.psum_pool(name="bank", bufs=TRANSPOSE_BANKS))
         y_pool = stack.enter_context(tc.psum_pool(name="y", bufs=Y_BANKS))
+        stack.enter_context(tc.manual_schedule())
 
         h_chunks = {}
 
         def load(c):
-            h_chunk = h_pool.tile([P, CHUNK_TILES, HOPS, FEATURES], BF16)
+            h_chunk = h_pool.tile([P, CHUNK_LAYERS, HOPS, FEATURES], BF16)
             nc.sync.dma_start(
-                out=h_chunk[:], in_=h_by_partition[:, c * CHUNK_TILES : (c + 1) * CHUNK_TILES, :, :]
+                out=h_chunk[:], in_=h_by_partition[:, c * CHUNK_LAYERS : (c + 1) * CHUNK_LAYERS, :, :]
             )
             h_chunks[c] = h_chunk
 
@@ -68,10 +76,10 @@ def tile_dogtaitujuanji_pb_t_kernel(
             nc.sync.dma_start(out=w_words[:, operand, :].bitcast(I32), in_=words[0, :, :].bitcast(I32))
 
         def load_scales(operand, scale_rows):
-            for r in range(4):
+            for r in range(QUADRANT_BLOCKS):
                 nc.sync.dma_start(
-                    out=w_planes[r:P:32, operand, :].bitcast(I32),
-                    in_=scale_rows[0, r:16:4, :].bitcast(I32),
+                    out=w_planes[r:P:QUADRANT, operand, :].bitcast(I32),
+                    in_=scale_rows[0, r:BLOCKS:QUADRANT_BLOCKS, :].bitcast(I32),
                 )
 
         load(0)
@@ -110,27 +118,27 @@ def tile_dogtaitujuanji_pb_t_kernel(
         scales_of = {}
 
         def add_hops(c):
-            hop_sum = mean_pool.tile([P, CHUNK_TILES, FEATURES], BF16)
+            hop_sum = mean_pool.tile([P, CHUNK_LAYERS, FEATURES], BF16)
             nc.vector.tensor_tensor(
                 out=hop_sum[:], in0=h_chunks[c][:, :, 1, :], in1=h_chunks[c][:, :, 2, :], op=ALU.add
             )
             hop_sum_of[c] = hop_sum
 
         def halve(c):
-            neigh = mean_pool.tile([P, CHUNK_TILES, FEATURES], BF16)
+            neigh = mean_pool.tile([P, CHUNK_LAYERS, FEATURES], BF16)
             nc.vector.tensor_scalar(out=neigh[:], in0=hop_sum_of[c][:], scalar1=0.5, scalar2=None, op0=ALU.mult)
             return neigh
 
         def features_to_partitions(item_rows, grouped):
-            grouped_words = grouped.bitcast(F32).rearrange("p (i u) -> p i u", u=2)
-            for pair in range(CHUNK_TILES // 2):
+            grouped_pairs = grouped.bitcast(F32).rearrange("p (i u) -> p i u", u=2)
+            for half_chunk in range(CHUNK_LAYERS // 2):
                 bank = bank_pool.tile([P, 2, 2 * P], F32, tag="bank")
                 for a in range(2):
-                    row_words = item_rows(2 * pair + a).bitcast(F32)
+                    row_pairs = item_rows(2 * half_chunk + a).bitcast(F32)
                     for u in range(2):
-                        nc.tensor.transpose(bank[:, u, a * P : (a + 1) * P], row_words[:, u:WORDS:2], ident[:])
+                        nc.tensor.transpose(bank[:, u, a * P : (a + 1) * P], row_pairs[:, u:PAIRS:2], ident[:])
                 nc.scalar.copy(
-                    out=grouped_words[:, 2 * pair * P : 2 * (pair + 1) * P, :],
+                    out=grouped_pairs[:, 2 * half_chunk * P : 2 * (half_chunk + 1) * P, :],
                     in_=bank[:].rearrange("p u i -> p i u"),
                 )
 
@@ -171,9 +179,8 @@ def tile_dogtaitujuanji_pb_t_kernel(
             nc.vector.bn_stats(out=stats[:, c, :], in_=y_of[c])
 
         add_hops(0)
-        for c in range(CHUNKS + 1):
-            if c < CHUNKS:
-                regroup(c, halve(c))
+        for c in range(CHUNKS):
+            regroup(c, halve(c))
             if c >= 1:
                 quantise(c - 1, NEIGH)
                 multiply(c - 1)
@@ -181,8 +188,7 @@ def tile_dogtaitujuanji_pb_t_kernel(
                 gather_statistics(c - 2)
             if c + 1 < CHUNKS:
                 add_hops(c + 1)
-            if c < CHUNKS:
-                quantise(c, SELF)
+            quantise(c, SELF)
 
         gb_bank = bank_pool.tile([P, P], BF16, tag="bank")
         nc.tensor.transpose(gb_bank[:], gb_rows[:], ident_bf[:])
@@ -193,6 +199,9 @@ def tile_dogtaitujuanji_pb_t_kernel(
         minus_gamma = keep.tile([P, 1], F32)
         nc.vector.tensor_scalar(out=minus_gamma[:], in0=gamma_col, scalar1=-1.0, scalar2=None, op0=ALU.mult)
 
+        quantise(CHUNKS - 1, NEIGH)
+        multiply(CHUNKS - 1)
+        gather_statistics(CHUNKS - 2)
         gather_statistics(CHUNKS - 1)
 
         mean_var = keep.tile([P, 2], F32)
@@ -210,13 +219,13 @@ def tile_dogtaitujuanji_pb_t_kernel(
             out=shift[:], in0=minus_mean_gamma[:], scalar=inv_std[:, 0:1], in1=beta_col, op0=ALU.mult, op1=ALU.add
         )
 
-        out_rows = keep.tile([P, TILES, OUT_COLS], F32)
+        out_rows = keep.tile([P, LAYERS, OUT_COLS], F32)
         for c in range(CHUNKS):
             sig = out_pool.tile([P, CHUNK_ITEMS], F32)
             nc.scalar.activation(out=sig[:], in_=y_of[c], func=ACT.Sigmoid, bias=shift[:, 0:1], scale=slope[:, 0:1])
-            out_bank = bank_pool.tile([P, CHUNK_TILES, OUT_COLS], F32, tag="bank")
-            for a in range(CHUNK_TILES):
+            out_bank = bank_pool.tile([P, CHUNK_LAYERS, OUT_COLS], F32, tag="bank")
+            for a in range(CHUNK_LAYERS):
                 nc.tensor.transpose(out_bank[:, a, :], sig[:, a * P : (a + 1) * P], ident[:])
-            tiles = slice(c * CHUNK_TILES, (c + 1) * CHUNK_TILES)
-            nc.vector.tensor_copy(out=out_rows[:, tiles, :], in_=out_bank[:])
-            nc.sync.dma_start(out=out_by_partition[:, tiles, :], in_=out_rows[:, tiles, :])
+            layers = slice(c * CHUNK_LAYERS, (c + 1) * CHUNK_LAYERS)
+            nc.vector.tensor_copy(out=out_rows[:, layers, :], in_=out_bank[:])
+            nc.sync.dma_start(out=out_by_partition[:, layers, :], in_=out_rows[:, layers, :])

@@ -36,6 +36,10 @@ PSUM_BANKS = 8
 Y_BANKS = 2
 TRANSPOSE_BANKS = PSUM_BANKS - Y_BANKS
 
+SCALAR_STATS_CHUNKS = 6
+SCALAR_STATS_ITEMS = SCALAR_STATS_CHUNKS * CHUNK_ITEMS
+VECTOR_STATS_CHUNKS = CHUNKS - SCALAR_STATS_CHUNKS
+
 SELF = 0
 NEIGH = 1
 
@@ -110,7 +114,10 @@ def tile_dogtaitujuanji_pb_t_kernel(
 
         y_sbuf = keep.tile([P, (CHUNKS - Y_BANKS) * CHUNK_ITEMS], F32)
         y_of = {}
-        stats = keep.tile([P, CHUNKS, BN_STATS_DIM], F32)
+        stats = keep.tile([P, VECTOR_STATS_CHUNKS * BN_STATS_DIM + 3], F32)
+        sums = keep.tile([P, 2, SCALAR_STATS_CHUNKS], F32)
+        minus_pivot = keep.tile([P, 1], F32)
+        squares = keep.tile([P, CHUNK_ITEMS], F32)
 
         hop_sum_of = {}
         grouped_of = {}
@@ -169,14 +176,52 @@ def tile_dogtaitujuanji_pb_t_kernel(
                     start=(operand == SELF),
                     stop=(operand == NEIGH),
                 )
-            if c < CHUNKS - Y_BANKS:
+            if c < SCALAR_STATS_CHUNKS:
+                y_of[c] = y_sbuf[:, c * CHUNK_ITEMS : (c + 1) * CHUNK_ITEMS]
+                nc.scalar.activation(out=y_of[c], in_=y_bank[:], func=ACT.Copy, accum_out=sums[:, 0, c : c + 1])
+                if c == 0:
+                    nc.gpsimd.tensor_scalar(
+                        out=minus_pivot[:], in0=sums[:, 0, 0:1], scalar1=-1.0 / CHUNK_ITEMS, scalar2=None, op0=ALU.mult
+                    )
+            elif c < CHUNKS - Y_BANKS:
                 y_of[c] = y_sbuf[:, c * CHUNK_ITEMS : (c + 1) * CHUNK_ITEMS]
                 nc.scalar.copy(out=y_of[c], in_=y_bank[:])
             else:
                 y_of[c] = y_bank[:]
 
         def gather_statistics(c):
-            nc.vector.bn_stats(out=stats[:, c, :], in_=y_of[c])
+            if c < SCALAR_STATS_CHUNKS:
+                nc.scalar.activation(
+                    out=squares[:], in_=y_of[c], func=ACT.Square, bias=minus_pivot[:, 0:1], scale=1.0,
+                    accum_out=sums[:, 1, c : c + 1],
+                )
+            else:
+                v = c - SCALAR_STATS_CHUNKS
+                nc.vector.bn_stats(out=stats[:, v * BN_STATS_DIM : (v + 1) * BN_STATS_DIM], in_=y_of[c])
+
+        totals = keep.tile([P, 2], F32)
+        triple = keep.tile([P, 3], F32)
+        nc.gpsimd.memset(triple[:, 0:1], float(SCALAR_STATS_ITEMS))
+
+        def total_scalar_statistics():
+            nc.vector.tensor_reduce(out=totals[:], in_=sums[:], op=ALU.add, axis=mybir.AxisListType.X)
+            nc.gpsimd.tensor_scalar(
+                out=triple[:, 1:2], in0=totals[:, 0:1], scalar1=1.0 / SCALAR_STATS_ITEMS, scalar2=None, op0=ALU.mult
+            )
+            off_pivot = keep.tile([P, 1], F32)
+            nc.gpsimd.tensor_scalar(
+                out=off_pivot[:], in0=totals[:, 0:1], scalar1=1.0 / SCALAR_STATS_ITEMS, scalar2=minus_pivot[:, 0:1],
+                op0=ALU.mult, op1=ALU.add,
+            )
+            off_pivot_squared = keep.tile([P, 1], F32)
+            nc.gpsimd.tensor_tensor(out=off_pivot_squared[:], in0=off_pivot[:], in1=off_pivot[:], op=ALU.mult)
+            nc.gpsimd.tensor_scalar(
+                out=triple[:, 2:3], in0=off_pivot_squared[:], scalar1=-float(SCALAR_STATS_ITEMS), scalar2=totals[:, 1:2],
+                op0=ALU.mult, op1=ALU.add,
+            )
+
+        def file_scalar_statistics():
+            nc.vector.tensor_copy(out=stats[:, VECTOR_STATS_CHUNKS * BN_STATS_DIM :], in_=triple[:])
 
         add_hops(0)
         for c in range(CHUNKS):
@@ -186,6 +231,10 @@ def tile_dogtaitujuanji_pb_t_kernel(
                 multiply(c - 1)
             if c >= 2:
                 gather_statistics(c - 2)
+            if c == SCALAR_STATS_CHUNKS + 2:
+                total_scalar_statistics()
+            if c == SCALAR_STATS_CHUNKS + 3:
+                file_scalar_statistics()
             if c + 1 < CHUNKS:
                 add_hops(c + 1)
             quantise(c, SELF)
@@ -205,7 +254,7 @@ def tile_dogtaitujuanji_pb_t_kernel(
         gather_statistics(CHUNKS - 1)
 
         mean_var = keep.tile([P, 2], F32)
-        nc.vector.bn_aggr(out=mean_var[:], in_=stats[:].rearrange("p c s -> p (c s)"))
+        nc.vector.bn_aggr(out=mean_var[:], in_=stats[:])
         var_eps = keep.tile([P, 1], F32)
         nc.vector.tensor_scalar(out=var_eps[:], in0=mean_var[:, 1:2], scalar1=BN_EPS, scalar2=None, op0=ALU.add)
         inv_std = keep.tile([P, 1], F32)

@@ -104,13 +104,11 @@ def tile_dogtaitujuanji_pb_t_kernel(
         make_identity(nc, ident[:])
         ident_bf = keep.tile([P, P], BF16)
         nc.vector.tensor_copy(out=ident_bf[:], in_=ident[:])
-        minus_half = keep.tile([P, 1], F32)
-        nc.vector.memset(minus_half[:], -0.5)
 
         gb_rows = keep.tile([P, P], BF16)
         nc.vector.memset(gb_rows[:], 0.0)
         nc.gpsimd.dma_start(out=gb_rows[0:1, :], in_=gamma.rearrange("(o f) -> o f", o=1))
-        nc.gpsimd.dma_start(out=gb_rows[1:2, :], in_=beta.rearrange("(o f) -> o f", o=1))
+        nc.gpsimd.dma_start(out=gb_rows[3:4, :], in_=beta.rearrange("(o f) -> o f", o=1))
 
         y_sbuf = keep.tile([P, (CHUNKS - Y_BANKS) * CHUNK_ITEMS], F32)
         y_of = {}
@@ -241,12 +239,8 @@ def tile_dogtaitujuanji_pb_t_kernel(
 
         gb_bank = bank_pool.tile([P, P], BF16, tag="bank")
         nc.tensor.transpose(gb_bank[:], gb_rows[:], ident_bf[:])
-        gamma_beta = keep.tile([P, 2], F32)
-        nc.vector.tensor_copy(out=gamma_beta[:], in_=gb_bank[:, 0:2])
-        gamma_col = gamma_beta[:, 0:1]
-        beta_col = gamma_beta[:, 1:2]
-        minus_gamma = keep.tile([P, 1], F32)
-        nc.vector.tensor_scalar(out=minus_gamma[:], in0=gamma_col, scalar1=-1.0, scalar2=None, op0=ALU.mult)
+        gb_cols = keep.tile([P, 4], F32)
+        nc.vector.tensor_copy(out=gb_cols[:], in_=gb_bank[:, 0:4])
 
         quantise(CHUNKS - 1, NEIGH)
         multiply(CHUNKS - 1)
@@ -255,26 +249,27 @@ def tile_dogtaitujuanji_pb_t_kernel(
 
         mean_var = keep.tile([P, 2], F32)
         nc.vector.bn_aggr(out=mean_var[:], in_=stats[:])
-        var_eps = keep.tile([P, 1], F32)
-        nc.vector.tensor_scalar(out=var_eps[:], in0=mean_var[:, 1:2], scalar1=BN_EPS, scalar2=None, op0=ALU.add)
         inv_std = keep.tile([P, 1], F32)
-        nc.gpsimd.tensor_tensor(out=inv_std[:], in0=var_eps[:], in1=minus_half[:], op=ALU.pow)
-        minus_mean_gamma = keep.tile([P, 1], F32)
-        nc.vector.tensor_tensor(out=minus_mean_gamma[:], in0=mean_var[:, 0:1], in1=minus_gamma[:], op=ALU.mult)
-        slope = keep.tile([P, 1], F32)
-        nc.vector.tensor_tensor(out=slope[:], in0=gamma_col, in1=inv_std[:], op=ALU.mult)
-        shift = keep.tile([P, 1], F32)
+        nc.scalar.activation(out=inv_std[:], in_=mean_var[:, 1:2], func=ACT.Abs_reciprocal_sqrt, bias=BN_EPS, scale=1.0)
         nc.vector.scalar_tensor_tensor(
-            out=shift[:], in0=minus_mean_gamma[:], scalar=inv_std[:, 0:1], in1=beta_col, op0=ALU.mult, op1=ALU.add
+            out=gb_cols[:, 1:2], in0=mean_var[:, 0:1], scalar=-1.0, in1=gb_cols[:, 0:1], op0=ALU.mult, op1=ALU.mult
         )
+        slope_shift = keep.tile([P, 2], F32)
+        nc.vector.scalar_tensor_tensor(
+            out=slope_shift[:], in0=gb_cols[:, 0:2], scalar=inv_std[:, 0:1], in1=gb_cols[:, 2:4], op0=ALU.mult, op1=ALU.add
+        )
+        slope = slope_shift[:, 0:1]
+        shift = slope_shift[:, 1:2]
 
         out_rows = keep.tile([P, LAYERS, OUT_COLS], F32)
         for c in range(CHUNKS):
-            sig = out_pool.tile([P, CHUNK_ITEMS], F32)
-            nc.scalar.activation(out=sig[:], in_=y_of[c], func=ACT.Sigmoid, bias=shift[:, 0:1], scale=slope[:, 0:1])
-            out_bank = bank_pool.tile([P, CHUNK_LAYERS, OUT_COLS], F32, tag="bank")
+            z = out_pool.tile([P, CHUNK_ITEMS], F32)
+            nc.vector.tensor_scalar(
+                out=z[:], in0=y_of[c], scalar1=slope, scalar2=shift, op0=ALU.mult, op1=ALU.add
+            )
+            z_bank = bank_pool.tile([P, CHUNK_LAYERS, OUT_COLS], F32, tag="bank")
             for a in range(CHUNK_LAYERS):
-                nc.tensor.transpose(out_bank[:, a, :], sig[:, a * P : (a + 1) * P], ident[:])
+                nc.tensor.transpose(z_bank[:, a, :], z[:, a * P : (a + 1) * P], ident[:])
             layers = slice(c * CHUNK_LAYERS, (c + 1) * CHUNK_LAYERS)
-            nc.vector.tensor_copy(out=out_rows[:, layers, :], in_=out_bank[:])
+            nc.scalar.activation(out=out_rows[:, layers, :], in_=z_bank[:], func=ACT.Sigmoid)
             nc.sync.dma_start(out=out_by_partition[:, layers, :], in_=out_rows[:, layers, :])

@@ -36,9 +36,9 @@ PSUM_BANKS = 8
 Y_BANKS = 2
 TRANSPOSE_BANKS = PSUM_BANKS - Y_BANKS
 
-SCALAR_STATS_CHUNKS = 6
-SCALAR_STATS_ITEMS = SCALAR_STATS_CHUNKS * CHUNK_ITEMS
-VECTOR_STATS_CHUNKS = CHUNKS - SCALAR_STATS_CHUNKS
+SHARED_CHUNKS = 7
+SCALAR_PART = CHUNK_ITEMS // 2
+SCALAR_STATS_ITEMS = SHARED_CHUNKS * SCALAR_PART
 
 SELF = 0
 NEIGH = 1
@@ -112,10 +112,10 @@ def tile_dogtaitujuanji_pb_t_kernel(
 
         y_sbuf = keep.tile([P, (CHUNKS - Y_BANKS) * CHUNK_ITEMS], F32)
         y_of = {}
-        stats = keep.tile([P, VECTOR_STATS_CHUNKS * BN_STATS_DIM + 3], F32)
-        sums = keep.tile([P, 2, SCALAR_STATS_CHUNKS], F32)
+        stats = keep.tile([P, CHUNKS * BN_STATS_DIM + 3], F32)
+        sums = keep.tile([P, 2, SHARED_CHUNKS], F32)
         minus_pivot = keep.tile([P, 1], F32)
-        squares = keep.tile([P, CHUNK_ITEMS], F32)
+        squares = keep.tile([P, SCALAR_PART], F32)
 
         hop_sum_of = {}
         grouped_of = {}
@@ -174,12 +174,16 @@ def tile_dogtaitujuanji_pb_t_kernel(
                     start=(operand == SELF),
                     stop=(operand == NEIGH),
                 )
-            if c < SCALAR_STATS_CHUNKS:
+            if c < SHARED_CHUNKS:
                 y_of[c] = y_sbuf[:, c * CHUNK_ITEMS : (c + 1) * CHUNK_ITEMS]
-                nc.scalar.activation(out=y_of[c], in_=y_bank[:], func=ACT.Copy, accum_out=sums[:, 0, c : c + 1])
+                nc.scalar.activation(
+                    out=y_of[c][:, 0:SCALAR_PART], in_=y_bank[:, 0:SCALAR_PART], func=ACT.Copy,
+                    accum_out=sums[:, 0, c : c + 1],
+                )
+                nc.scalar.copy(out=y_of[c][:, SCALAR_PART:], in_=y_bank[:, SCALAR_PART:])
                 if c == 0:
                     nc.gpsimd.tensor_scalar(
-                        out=minus_pivot[:], in0=sums[:, 0, 0:1], scalar1=-1.0 / CHUNK_ITEMS, scalar2=None, op0=ALU.mult
+                        out=minus_pivot[:], in0=sums[:, 0, 0:1], scalar1=-1.0 / SCALAR_PART, scalar2=None, op0=ALU.mult
                     )
             elif c < CHUNKS - Y_BANKS:
                 y_of[c] = y_sbuf[:, c * CHUNK_ITEMS : (c + 1) * CHUNK_ITEMS]
@@ -188,14 +192,14 @@ def tile_dogtaitujuanji_pb_t_kernel(
                 y_of[c] = y_bank[:]
 
         def gather_statistics(c):
-            if c < SCALAR_STATS_CHUNKS:
+            vector_part = y_of[c]
+            if c < SHARED_CHUNKS:
                 nc.scalar.activation(
-                    out=squares[:], in_=y_of[c], func=ACT.Square, bias=minus_pivot[:, 0:1], scale=1.0,
+                    out=squares[:], in_=y_of[c][:, 0:SCALAR_PART], func=ACT.Square, bias=minus_pivot[:, 0:1], scale=1.0,
                     accum_out=sums[:, 1, c : c + 1],
                 )
-            else:
-                v = c - SCALAR_STATS_CHUNKS
-                nc.vector.bn_stats(out=stats[:, v * BN_STATS_DIM : (v + 1) * BN_STATS_DIM], in_=y_of[c])
+                vector_part = y_of[c][:, SCALAR_PART:]
+            nc.vector.bn_stats(out=stats[:, c * BN_STATS_DIM : (c + 1) * BN_STATS_DIM], in_=vector_part)
 
         totals = keep.tile([P, 2], F32)
         triple = keep.tile([P, 3], F32)
@@ -219,7 +223,7 @@ def tile_dogtaitujuanji_pb_t_kernel(
             )
 
         def file_scalar_statistics():
-            nc.vector.tensor_copy(out=stats[:, VECTOR_STATS_CHUNKS * BN_STATS_DIM :], in_=triple[:])
+            nc.vector.tensor_copy(out=stats[:, CHUNKS * BN_STATS_DIM :], in_=triple[:])
 
         add_hops(0)
         for c in range(CHUNKS):
@@ -229,10 +233,8 @@ def tile_dogtaitujuanji_pb_t_kernel(
                 multiply(c - 1)
             if c >= 2:
                 gather_statistics(c - 2)
-            if c == SCALAR_STATS_CHUNKS + 2:
+            if c == SHARED_CHUNKS + 2:
                 total_scalar_statistics()
-            if c == SCALAR_STATS_CHUNKS + 3:
-                file_scalar_statistics()
             if c + 1 < CHUNKS:
                 add_hops(c + 1)
             quantise(c, SELF)
@@ -245,6 +247,7 @@ def tile_dogtaitujuanji_pb_t_kernel(
         quantise(CHUNKS - 1, NEIGH)
         multiply(CHUNKS - 1)
         gather_statistics(CHUNKS - 2)
+        file_scalar_statistics()
         gather_statistics(CHUNKS - 1)
 
         mean_var = keep.tile([P, 2], F32)

@@ -36,7 +36,7 @@ PSUM_BANKS = 8
 Y_BANKS = 2
 TRANSPOSE_BANKS = PSUM_BANKS - Y_BANKS
 
-SHARED_CHUNKS = 7
+SHARED_CHUNKS = CHUNKS - Y_BANKS
 SCALAR_PART = CHUNK_ITEMS // 2
 SCALAR_STATS_ITEMS = SHARED_CHUNKS * SCALAR_PART
 
@@ -110,7 +110,7 @@ def tile_dogtaitujuanji_pb_t_kernel(
         nc.gpsimd.dma_start(out=gb_rows[0:1, :], in_=gamma.rearrange("(o f) -> o f", o=1))
         nc.gpsimd.dma_start(out=gb_rows[3:4, :], in_=beta.rearrange("(o f) -> o f", o=1))
 
-        y_sbuf = keep.tile([P, (CHUNKS - Y_BANKS) * CHUNK_ITEMS], F32)
+        y_sbuf = keep.tile([P, SHARED_CHUNKS * CHUNK_ITEMS], F32)
         y_of = {}
         stats = keep.tile([P, CHUNKS * BN_STATS_DIM + 3], F32)
         sums = keep.tile([P, 2, SHARED_CHUNKS], F32)
@@ -182,12 +182,7 @@ def tile_dogtaitujuanji_pb_t_kernel(
                 )
                 nc.scalar.copy(out=y_of[c][:, SCALAR_PART:], in_=y_bank[:, SCALAR_PART:])
                 if c == 0:
-                    nc.gpsimd.tensor_scalar(
-                        out=minus_pivot[:], in0=sums[:, 0, 0:1], scalar1=-1.0 / SCALAR_PART, scalar2=None, op0=ALU.mult
-                    )
-            elif c < CHUNKS - Y_BANKS:
-                y_of[c] = y_sbuf[:, c * CHUNK_ITEMS : (c + 1) * CHUNK_ITEMS]
-                nc.scalar.copy(out=y_of[c], in_=y_bank[:])
+                    nc.scalar.activation(out=minus_pivot[:], in_=sums[:, 0, 0:1], func=ACT.Copy, scale=-1.0 / SCALAR_PART)
             else:
                 y_of[c] = y_bank[:]
 
@@ -201,53 +196,48 @@ def tile_dogtaitujuanji_pb_t_kernel(
                 vector_part = y_of[c][:, SCALAR_PART:]
             nc.vector.bn_stats(out=stats[:, c * BN_STATS_DIM : (c + 1) * BN_STATS_DIM], in_=vector_part)
 
+        triple = stats[:, CHUNKS * BN_STATS_DIM : CHUNKS * BN_STATS_DIM + 3]
+        nc.vector.memset(triple[:, 0:1], float(SCALAR_STATS_ITEMS))
         totals = keep.tile([P, 2], F32)
-        triple = keep.tile([P, 3], F32)
-        nc.gpsimd.memset(triple[:, 0:1], float(SCALAR_STATS_ITEMS))
+        summed = keep.tile([P, SHARED_CHUNKS], F32)
+        off_pivot_squared = keep.tile([P, 1], F32)
 
-        def total_scalar_statistics():
-            nc.vector.tensor_reduce(out=totals[:], in_=sums[:], op=ALU.add, axis=mybir.AxisListType.X)
-            nc.gpsimd.tensor_scalar(
-                out=triple[:, 1:2], in0=totals[:, 0:1], scalar1=1.0 / SCALAR_STATS_ITEMS, scalar2=None, op0=ALU.mult
+        def work_up_scalar_statistics():
+            for row in range(2):
+                nc.scalar.activation(out=summed[:], in_=sums[:, row, :], func=ACT.Copy, accum_out=totals[:, row : row + 1])
+            nc.scalar.activation(out=triple[:, 1:2], in_=totals[:, 0:1], func=ACT.Copy, scale=1.0 / SCALAR_STATS_ITEMS)
+            nc.scalar.activation(
+                out=off_pivot_squared[:], in_=totals[:, 0:1], func=ACT.Square, scale=1.0 / SCALAR_STATS_ITEMS,
+                bias=minus_pivot[:, 0:1],
             )
-            off_pivot = keep.tile([P, 1], F32)
-            nc.gpsimd.tensor_scalar(
-                out=off_pivot[:], in0=totals[:, 0:1], scalar1=1.0 / SCALAR_STATS_ITEMS, scalar2=minus_pivot[:, 0:1],
-                op0=ALU.mult, op1=ALU.add,
-            )
-            off_pivot_squared = keep.tile([P, 1], F32)
-            nc.gpsimd.tensor_tensor(out=off_pivot_squared[:], in0=off_pivot[:], in1=off_pivot[:], op=ALU.mult)
-            nc.gpsimd.tensor_scalar(
-                out=triple[:, 2:3], in0=off_pivot_squared[:], scalar1=-float(SCALAR_STATS_ITEMS), scalar2=totals[:, 1:2],
-                op0=ALU.mult, op1=ALU.add,
+            nc.scalar.activation(
+                out=triple[:, 2:3], in_=off_pivot_squared[:], func=ACT.Identity, scale=-float(SCALAR_STATS_ITEMS),
+                bias=totals[:, 1:2],
             )
 
-        def file_scalar_statistics():
-            nc.vector.tensor_copy(out=stats[:, CHUNKS * BN_STATS_DIM :], in_=triple[:])
-
+        gb_cols = keep.tile([P, 4], F32)
+        gb_bank_of = {}
         add_hops(0)
         for c in range(CHUNKS):
             regroup(c, halve(c))
+            if c == 2:
+                gb_bank_of[0] = bank_pool.tile([P, P], BF16, tag="bank", name="gb_bank")
+                nc.tensor.transpose(gb_bank_of[0][:], gb_rows[:], ident_bf[:])
+            if c == 3:
+                nc.vector.tensor_copy(out=gb_cols[:], in_=gb_bank_of[0][:, 0:4])
             if c >= 1:
                 quantise(c - 1, NEIGH)
                 multiply(c - 1)
             if c >= 2:
                 gather_statistics(c - 2)
-            if c == SHARED_CHUNKS + 2:
-                total_scalar_statistics()
             if c + 1 < CHUNKS:
                 add_hops(c + 1)
             quantise(c, SELF)
 
-        gb_bank = bank_pool.tile([P, P], BF16, tag="bank")
-        nc.tensor.transpose(gb_bank[:], gb_rows[:], ident_bf[:])
-        gb_cols = keep.tile([P, 4], F32)
-        nc.vector.tensor_copy(out=gb_cols[:], in_=gb_bank[:, 0:4])
-
         quantise(CHUNKS - 1, NEIGH)
         multiply(CHUNKS - 1)
+        work_up_scalar_statistics()
         gather_statistics(CHUNKS - 2)
-        file_scalar_statistics()
         gather_statistics(CHUNKS - 1)
 
         mean_var = keep.tile([P, 2], F32)

@@ -162,6 +162,13 @@ def tile_dogtaitujuanji_pb_t_kernel(
                 in_=grouped_of[c][:, operand, :],
             )
 
+        def quantise_both(c):
+            nc.vector.quantize_mx(
+                out=codes_of[c][:].rearrange("p o i -> p (o i)").bitcast(FP8X4),
+                scales=scales_of[c][:].rearrange("p o i -> p (o i)"),
+                in_=grouped_of[c][:].rearrange("p o i -> p (o i)"),
+            )
+
         def multiply(c):
             y_bank = y_pool.tile([P, CHUNK_ITEMS], F32)
             for operand in (SELF, NEIGH):
@@ -226,13 +233,13 @@ def tile_dogtaitujuanji_pb_t_kernel(
             if c == 3:
                 nc.vector.tensor_copy(out=gb_cols[:], in_=gb_bank_of[0][:, 0:4])
             if c >= 1:
-                quantise(c - 1, NEIGH)
+                quantise_both(c - 1)
                 multiply(c - 1)
-            if c >= 2:
-                gather_statistics(c - 2)
             if c + 1 < CHUNKS:
                 add_hops(c + 1)
-            quantise(c, SELF)
+            if c >= 2:
+                gather_statistics(c - 2)
+        quantise(CHUNKS - 1, SELF)
 
         quantise(CHUNKS - 1, NEIGH)
         multiply(CHUNKS - 1)

@@ -36,9 +36,11 @@ PSUM_BANKS = 8
 Y_BANKS = 2
 TRANSPOSE_BANKS = PSUM_BANKS - Y_BANKS
 
-SHARED_CHUNKS = CHUNKS - Y_BANKS
-SCALAR_PART = CHUNK_ITEMS // 2
-SCALAR_STATS_ITEMS = SHARED_CHUNKS * SCALAR_PART
+COPIED_CHUNKS = CHUNKS - Y_BANKS
+SCALAR_PART = (CHUNK_ITEMS // 2,) * (COPIED_CHUNKS - 1) + (CHUNK_ITEMS,) + (0,) * Y_BANKS
+SCALAR_STATS_ITEMS = sum(SCALAR_PART)
+SCALAR_CHUNKS = tuple(c for c in range(CHUNKS) if SCALAR_PART[c] > 0)
+VECTOR_CHUNKS = tuple(c for c in range(CHUNKS) if SCALAR_PART[c] < CHUNK_ITEMS)
 
 SELF = 0
 NEIGH = 1
@@ -55,7 +57,7 @@ def tile_dogtaitujuanji_pb_t_kernel(
 
     with ExitStack() as stack:
         keep = stack.enter_context(tc.tile_pool(name="keep", bufs=1))
-        h_pool = stack.enter_context(tc.tile_pool(name="h", bufs=CHUNKS))
+        h_pool = stack.enter_context(tc.tile_pool(name="h", bufs=CHUNKS - 1))
         mean_pool = stack.enter_context(tc.tile_pool(name="mean", bufs=2))
         mx_pool = stack.enter_context(tc.tile_pool(name="mx", bufs=3))
         out_pool = stack.enter_context(tc.tile_pool(name="out", bufs=4))
@@ -63,14 +65,23 @@ def tile_dogtaitujuanji_pb_t_kernel(
         y_pool = stack.enter_context(tc.psum_pool(name="y", bufs=Y_BANKS))
         stack.enter_context(tc.manual_schedule())
 
-        h_chunks = {}
+        hop_of = {}
 
         def load(c):
-            h_chunk = h_pool.tile([P, CHUNK_LAYERS, HOPS, FEATURES], BF16)
-            nc.sync.dma_start(
-                out=h_chunk[:], in_=h_by_partition[:, c * CHUNK_LAYERS : (c + 1) * CHUNK_LAYERS, :, :]
-            )
-            h_chunks[c] = h_chunk
+            rows = h_by_partition[:, c * CHUNK_LAYERS : (c + 1) * CHUNK_LAYERS, :, :]
+            if c < CHUNKS - 1:
+                h_chunk = h_pool.tile([P, CHUNK_LAYERS, HOPS, FEATURES], BF16)
+                nc.sync.dma_start(out=h_chunk[:], in_=rows)
+                for q in range(HOPS):
+                    hop_of[c, q] = h_chunk[:, :, q, :]
+            else:
+                last_others = keep.tile([P, CHUNK_LAYERS, HOPS - 1, FEATURES], BF16)
+                last_self = keep.tile([P, CHUNK_LAYERS, FEATURES], BF16)
+                nc.sync.dma_start(out=last_others[:], in_=rows[:, :, 1:HOPS, :])
+                nc.sync.dma_start(out=last_self[:], in_=rows[:, :, 0, :])
+                hop_of[c, 0] = last_self[:]
+                for q in range(1, HOPS):
+                    hop_of[c, q] = last_others[:, :, q - 1, :]
 
         w_words = keep.tile([P, 2, 2 * OUT_COLS], U8, align_bytes=64)
         w_planes = keep.tile([P, 2, OUT_COLS], U8, align_bytes=64)
@@ -97,8 +108,8 @@ def tile_dogtaitujuanji_pb_t_kernel(
 
         table_in = keep.tile([P, 1], F32)
         table_out = keep.tile([P, 1], F32)
-        nc.vector.memset(table_in[:], 0.0)
-        nc.scalar.activation(out=table_out[:], in_=table_in[:], func=ACT.Sigmoid)
+        nc.vector.memset(table_in[:], 1.0)
+        nc.scalar.activation(out=table_out[:], in_=table_in[:], func=ACT.Abs_reciprocal_sqrt)
 
         ident = keep.tile([P, P], F32)
         make_identity(nc, ident[:])
@@ -110,12 +121,12 @@ def tile_dogtaitujuanji_pb_t_kernel(
         nc.gpsimd.dma_start(out=gb_rows[0:1, :], in_=gamma.rearrange("(o f) -> o f", o=1))
         nc.gpsimd.dma_start(out=gb_rows[3:4, :], in_=beta.rearrange("(o f) -> o f", o=1))
 
-        y_sbuf = keep.tile([P, SHARED_CHUNKS * CHUNK_ITEMS], F32)
+        y_sbuf = keep.tile([P, COPIED_CHUNKS * CHUNK_ITEMS], F32)
         y_of = {}
-        stats = keep.tile([P, CHUNKS * BN_STATS_DIM + 3], F32)
-        sums = keep.tile([P, 2, SHARED_CHUNKS], F32)
+        stats = keep.tile([P, len(VECTOR_CHUNKS) * BN_STATS_DIM + 3], F32)
+        sums = keep.tile([P, 2, len(SCALAR_CHUNKS)], F32)
         minus_pivot = keep.tile([P, 1], F32)
-        squares = keep.tile([P, SCALAR_PART], F32)
+        squares = keep.tile([P, CHUNK_ITEMS], F32)
 
         hop_sum_of = {}
         grouped_of = {}
@@ -125,7 +136,7 @@ def tile_dogtaitujuanji_pb_t_kernel(
         def add_hops(c):
             hop_sum = mean_pool.tile([P, CHUNK_LAYERS, FEATURES], BF16)
             nc.vector.tensor_tensor(
-                out=hop_sum[:], in0=h_chunks[c][:, :, 1, :], in1=h_chunks[c][:, :, 2, :], op=ALU.add
+                out=hop_sum[:], in0=hop_of[c, 1], in1=hop_of[c, 2], op=ALU.add
             )
             hop_sum_of[c] = hop_sum
 
@@ -149,7 +160,7 @@ def tile_dogtaitujuanji_pb_t_kernel(
 
         def regroup(c, neigh):
             grouped = mx_pool.tile([P, 2, CHUNK_ITEMS * PACK], BF16, align_bytes=64)
-            features_to_partitions(lambda a: h_chunks[c][:, a, 0, :], grouped[:, SELF, :])
+            features_to_partitions(lambda a: hop_of[c, 0][:, a, :], grouped[:, SELF, :])
             features_to_partitions(lambda a: neigh[:, a, :], grouped[:, NEIGH, :])
             grouped_of[c] = grouped
             codes_of[c] = mx_pool.tile([P, 2, CHUNK_ITEMS], U32, align_bytes=64, name="codes")
@@ -181,32 +192,37 @@ def tile_dogtaitujuanji_pb_t_kernel(
                     start=(operand == SELF),
                     stop=(operand == NEIGH),
                 )
-            if c < SHARED_CHUNKS:
-                y_of[c] = y_sbuf[:, c * CHUNK_ITEMS : (c + 1) * CHUNK_ITEMS]
-                nc.scalar.activation(
-                    out=y_of[c][:, 0:SCALAR_PART], in_=y_bank[:, 0:SCALAR_PART], func=ACT.Copy,
-                    accum_out=sums[:, 0, c : c + 1],
-                )
-                nc.scalar.copy(out=y_of[c][:, SCALAR_PART:], in_=y_bank[:, SCALAR_PART:])
-                if c == 0:
-                    nc.scalar.activation(out=minus_pivot[:], in_=sums[:, 0, 0:1], func=ACT.Copy, scale=-1.0 / SCALAR_PART)
-            else:
+            if c >= COPIED_CHUNKS:
                 y_of[c] = y_bank[:]
+                return
+            y_of[c] = y_sbuf[:, c * CHUNK_ITEMS : (c + 1) * CHUNK_ITEMS]
+            part = SCALAR_PART[c]
+            if part > 0:
+                s = SCALAR_CHUNKS.index(c)
+                nc.scalar.activation(
+                    out=y_of[c][:, 0:part], in_=y_bank[:, 0:part], func=ACT.Copy, accum_out=sums[:, 0, s : s + 1]
+                )
+                if s == 0:
+                    nc.scalar.activation(out=minus_pivot[:], in_=sums[:, 0, 0:1], func=ACT.Copy, scale=-1.0 / part)
+            if part < CHUNK_ITEMS:
+                nc.scalar.copy(out=y_of[c][:, part:], in_=y_bank[:, part:])
 
         def gather_statistics(c):
-            vector_part = y_of[c]
-            if c < SHARED_CHUNKS:
+            part = SCALAR_PART[c]
+            if part > 0:
+                s = SCALAR_CHUNKS.index(c)
                 nc.scalar.activation(
-                    out=squares[:], in_=y_of[c][:, 0:SCALAR_PART], func=ACT.Square, bias=minus_pivot[:, 0:1], scale=1.0,
-                    accum_out=sums[:, 1, c : c + 1],
+                    out=squares[:, 0:part], in_=y_of[c][:, 0:part], func=ACT.Square, bias=minus_pivot[:, 0:1], scale=1.0,
+                    accum_out=sums[:, 1, s : s + 1],
                 )
-                vector_part = y_of[c][:, SCALAR_PART:]
-            nc.vector.bn_stats(out=stats[:, c * BN_STATS_DIM : (c + 1) * BN_STATS_DIM], in_=vector_part)
+            if part < CHUNK_ITEMS:
+                v = VECTOR_CHUNKS.index(c)
+                nc.vector.bn_stats(out=stats[:, v * BN_STATS_DIM : (v + 1) * BN_STATS_DIM], in_=y_of[c][:, part:])
 
-        triple = stats[:, CHUNKS * BN_STATS_DIM : CHUNKS * BN_STATS_DIM + 3]
+        triple = stats[:, len(VECTOR_CHUNKS) * BN_STATS_DIM : len(VECTOR_CHUNKS) * BN_STATS_DIM + 3]
         nc.vector.memset(triple[:, 0:1], float(SCALAR_STATS_ITEMS))
         totals = keep.tile([P, 2], F32)
-        summed = keep.tile([P, SHARED_CHUNKS], F32)
+        summed = keep.tile([P, len(SCALAR_CHUNKS)], F32)
         off_pivot_squared = keep.tile([P, 1], F32)
 
         def work_up_scalar_statistics():

from contextlib import ExitStack

import concourse.mybir as mybir
from concourse.masks import make_identity

F32 = mybir.dt.float32
BF16 = mybir.dt.bfloat16
I32 = mybir.dt.int32
U32 = mybir.dt.uint32
U8 = mybir.dt.uint8
FP8X4 = mybir.dt.float8_e4m3fn_x4
FP4X4 = mybir.dt.float4_e2m1fn_x4
ALU = mybir.AluOpType
ACT = mybir.ActivationFunctionType

P = 128
ITEMS = 5120
HOPS = 3
FEATURES = 512
OUT_COLS = 128
BN_EPS = 1e-5

PACK = 4
PAIRS = FEATURES // 2
QUADRANT = 32
BLOCKS = FEATURES // 32
QUADRANT_BLOCKS = QUADRANT // 8

LAYERS = ITEMS // P
CHUNK_LAYERS = 4
CHUNK_ITEMS = CHUNK_LAYERS * P
CHUNKS = LAYERS // CHUNK_LAYERS
BN_STATS_DIM = 6

PSUM_BANKS = 8
Y_BANKS = 2
TRANSPOSE_BANKS = PSUM_BANKS - Y_BANKS

COPIED_CHUNKS = CHUNKS - Y_BANKS
SCALAR_PART = (CHUNK_ITEMS // 2,) * (COPIED_CHUNKS - 1) + (CHUNK_ITEMS,) + (0,) * Y_BANKS
SCALAR_STATS_ITEMS = sum(SCALAR_PART)
SCALAR_CHUNKS = tuple(c for c in range(CHUNKS) if SCALAR_PART[c] > 0)
VECTOR_CHUNKS = tuple(c for c in range(CHUNKS) if SCALAR_PART[c] < CHUNK_ITEMS)

SELF = 0
NEIGH = 1

FLOPS = 2 * 2 * ITEMS * FEATURES * OUT_COLS


def tile_dogtaitujuanji_pb_t_kernel(
    tc, h_sage, w1b_words, w1b_scales, w2b_words, w2b_scales, gamma, beta, out
):
    nc = tc.nc
    h_by_partition = h_sage.rearrange("(p t) q k -> p t q k", t=LAYERS)
    out_by_partition = out.rearrange("(p t) f -> p t f", t=LAYERS)

    with ExitStack() as stack:
        keep = stack.enter_context(tc.tile_pool(name="keep", bufs=1))
        h_pool = stack.enter_context(tc.tile_pool(name="h", bufs=CHUNKS - 1))
        mean_pool = stack.enter_context(tc.tile_pool(name="mean", bufs=2))
        mx_pool = stack.enter_context(tc.tile_pool(name="mx", bufs=3))
        out_pool = stack.enter_context(tc.tile_pool(name="out", bufs=4))
        bank_pool = stack.enter_context(tc.psum_pool(name="bank", bufs=TRANSPOSE_BANKS))
        y_pool = stack.enter_context(tc.psum_pool(name="y", bufs=Y_BANKS))
        stack.enter_context(tc.manual_schedule())

        hop_of = {}

        def load(c):
            rows = h_by_partition[:, c * CHUNK_LAYERS : (c + 1) * CHUNK_LAYERS, :, :]
            if c < CHUNKS - 1:
                h_chunk = h_pool.tile([P, CHUNK_LAYERS, HOPS, FEATURES], BF16)
                nc.sync.dma_start(out=h_chunk[:], in_=rows)
                for q in range(HOPS):
                    hop_of[c, q] = h_chunk[:, :, q, :]
            else:
                last_others = keep.tile([P, CHUNK_LAYERS, HOPS - 1, FEATURES], BF16)
                last_self = keep.tile([P, CHUNK_LAYERS, FEATURES], BF16)
                nc.sync.dma_start(out=last_others[:], in_=rows[:, :, 1:HOPS, :])
                nc.sync.dma_start(out=last_self[:], in_=rows[:, :, 0, :])
                hop_of[c, 0] = last_self[:]
                for q in range(1, HOPS):
                    hop_of[c, q] = last_others[:, :, q - 1, :]

        w_words = keep.tile([P, 2, 2 * OUT_COLS], U8, align_bytes=64)
        w_planes = keep.tile([P, 2, OUT_COLS], U8, align_bytes=64)
        nc.vector.memset(w_planes[:].bitcast(I32), 0)

        def load_words(operand, words):
            nc.sync.dma_start(out=w_words[:, operand, :].bitcast(I32), in_=words[0, :, :].bitcast(I32))

        def load_scales(operand, scale_rows):
            for r in range(QUADRANT_BLOCKS):
                nc.sync.dma_start(
                    out=w_planes[r:P:QUADRANT, operand, :].bitcast(I32),
                    in_=scale_rows[0, r:BLOCKS:QUADRANT_BLOCKS, :].bitcast(I32),
                )

        load(0)
        load_words(SELF, w2b_words)
        load_scales(SELF, w2b_scales)
        load_words(NEIGH, w1b_words)
        load(1)
        load_scales(NEIGH, w1b_scales)
        for c in range(2, CHUNKS):
            load(c)

        table_in = keep.tile([P, 1], F32)
        table_out = keep.tile([P, 1], F32)
        nc.vector.memset(table_in[:], 1.0)
        nc.scalar.activation(out=table_out[:], in_=table_in[:], func=ACT.Abs_reciprocal_sqrt)

        ident = keep.tile([P, P], F32)
        make_identity(nc, ident[:])
        ident_bf = keep.tile([P, P], BF16)
        nc.vector.tensor_copy(out=ident_bf[:], in_=ident[:])

        gb_rows = keep.tile([P, P], BF16)
        nc.vector.memset(gb_rows[:], 0.0)
        nc.gpsimd.dma_start(out=gb_rows[0:1, :], in_=gamma.rearrange("(o f) -> o f", o=1))
        nc.gpsimd.dma_start(out=gb_rows[3:4, :], in_=beta.rearrange("(o f) -> o f", o=1))

        y_sbuf = keep.tile([P, COPIED_CHUNKS * CHUNK_ITEMS], F32)
        y_of = {}
        stats = keep.tile([P, len(VECTOR_CHUNKS) * BN_STATS_DIM + 3], F32)
        sums = keep.tile([P, 2, len(SCALAR_CHUNKS)], F32)
        minus_pivot = keep.tile([P, 1], F32)
        squares = keep.tile([P, CHUNK_ITEMS], F32)

        hop_sum_of = {}
        grouped_of = {}
        codes_of = {}
        scales_of = {}

        def add_hops(c):
            hop_sum = mean_pool.tile([P, CHUNK_LAYERS, FEATURES], BF16)
            nc.vector.tensor_tensor(
                out=hop_sum[:], in0=hop_of[c, 1], in1=hop_of[c, 2], op=ALU.add
            )
            hop_sum_of[c] = hop_sum

        def halve(c):
            neigh = mean_pool.tile([P, CHUNK_LAYERS, FEATURES], BF16)
            nc.vector.tensor_scalar(out=neigh[:], in0=hop_sum_of[c][:], scalar1=0.5, scalar2=None, op0=ALU.mult)
            return neigh

        def features_to_partitions(item_rows, grouped):
            grouped_pairs = grouped.bitcast(F32).rearrange("p (i u) -> p i u", u=2)
            for half_chunk in range(CHUNK_LAYERS // 2):
                bank = bank_pool.tile([P, 2, 2 * P], F32, tag="bank")
                for a in range(2):
                    row_pairs = item_rows(2 * half_chunk + a).bitcast(F32)
                    for u in range(2):
                        nc.tensor.transpose(bank[:, u, a * P : (a + 1) * P], row_pairs[:, u:PAIRS:2], ident[:])
                nc.scalar.copy(
                    out=grouped_pairs[:, 2 * half_chunk * P : 2 * (half_chunk + 1) * P, :],
                    in_=bank[:].rearrange("p u i -> p i u"),
                )

        def regroup(c, neigh):
            grouped = mx_pool.tile([P, 2, CHUNK_ITEMS * PACK], BF16, align_bytes=64)
            features_to_partitions(lambda a: hop_of[c, 0][:, a, :], grouped[:, SELF, :])
            features_to_partitions(lambda a: neigh[:, a, :], grouped[:, NEIGH, :])
            grouped_of[c] = grouped
            codes_of[c] = mx_pool.tile([P, 2, CHUNK_ITEMS], U32, align_bytes=64, name="codes")
            scales_of[c] = mx_pool.tile([P, 2, CHUNK_ITEMS], U8, align_bytes=64, name="scales")

        def quantise(c, operand):
            nc.vector.quantize_mx(
                out=codes_of[c][:, operand, :].bitcast(FP8X4),
                scales=scales_of[c][:, operand, :],
                in_=grouped_of[c][:, operand, :],
            )

        def quantise_both(c):
            nc.vector.quantize_mx(
                out=codes_of[c][:].rearrange("p o i -> p (o i)").bitcast(FP8X4),
                scales=scales_of[c][:].rearrange("p o i -> p (o i)"),
                in_=grouped_of[c][:].rearrange("p o i -> p (o i)"),
            )

        def multiply(c):
            y_bank = y_pool.tile([P, CHUNK_ITEMS], F32)
            for operand in (SELF, NEIGH):
                nc.tensor.matmul_mx(
                    out=y_bank[:],
                    lhsT=w_words[:, operand, :].bitcast(FP4X4),
                    lhsT_scale=w_planes[:, operand, :],
                    rhs=codes_of[c][:, operand, :].bitcast(FP8X4),
                    rhs_scale=scales_of[c][:, operand, :],
                    start=(operand == SELF),
                    stop=(operand == NEIGH),
                )
            if c >= COPIED_CHUNKS:
                y_of[c] = y_bank[:]
                return
            y_of[c] = y_sbuf[:, c * CHUNK_ITEMS : (c + 1) * CHUNK_ITEMS]
            part = SCALAR_PART[c]
            if part > 0:
                s = SCALAR_CHUNKS.index(c)
                nc.scalar.activation(
                    out=y_of[c][:, 0:part], in_=y_bank[:, 0:part], func=ACT.Copy, accum_out=sums[:, 0, s : s + 1]
                )
                if s == 0:
                    nc.scalar.activation(out=minus_pivot[:], in_=sums[:, 0, 0:1], func=ACT.Copy, scale=-1.0 / part)
            if part < CHUNK_ITEMS:
                nc.scalar.copy(out=y_of[c][:, part:], in_=y_bank[:, part:])

        def gather_statistics(c):
            part = SCALAR_PART[c]
            if part > 0:
                s = SCALAR_CHUNKS.index(c)
                nc.scalar.activation(
                    out=squares[:, 0:part], in_=y_of[c][:, 0:part], func=ACT.Square, bias=minus_pivot[:, 0:1], scale=1.0,
                    accum_out=sums[:, 1, s : s + 1],
                )
            if part < CHUNK_ITEMS:
                v = VECTOR_CHUNKS.index(c)
                nc.vector.bn_stats(out=stats[:, v * BN_STATS_DIM : (v + 1) * BN_STATS_DIM], in_=y_of[c][:, part:])

        triple = stats[:, len(VECTOR_CHUNKS) * BN_STATS_DIM : len(VECTOR_CHUNKS) * BN_STATS_DIM + 3]
        nc.vector.memset(triple[:, 0:1], float(SCALAR_STATS_ITEMS))
        totals = keep.tile([P, 2], F32)
        summed = keep.tile([P, len(SCALAR_CHUNKS)], F32)
        off_pivot_squared = keep.tile([P, 1], F32)

        def work_up_scalar_statistics():
            for row in range(2):
                nc.scalar.activation(out=summed[:], in_=sums[:, row, :], func=ACT.Copy, accum_out=totals[:, row : row + 1])
            nc.scalar.activation(out=triple[:, 1:2], in_=totals[:, 0:1], func=ACT.Copy, scale=1.0 / SCALAR_STATS_ITEMS)
            nc.scalar.activation(
                out=off_pivot_squared[:], in_=totals[:, 0:1], func=ACT.Square, scale=1.0 / SCALAR_STATS_ITEMS,
                bias=minus_pivot[:, 0:1],
            )
            nc.scalar.activation(
                out=triple[:, 2:3], in_=off_pivot_squared[:], func=ACT.Identity, scale=-float(SCALAR_STATS_ITEMS),
                bias=totals[:, 1:2],
            )

        gb_cols = keep.tile([P, 4], F32)
        gb_bank_of = {}
        add_hops(0)
        for c in range(CHUNKS):
            regroup(c, halve(c))
            if c == 2:
                gb_bank_of[0] = bank_pool.tile([P, P], BF16, tag="bank", name="gb_bank")
                nc.tensor.transpose(gb_bank_of[0][:], gb_rows[:], ident_bf[:])
            if c == 3:
                nc.vector.tensor_copy(out=gb_cols[:], in_=gb_bank_of[0][:, 0:4])
            if c >= 1:
                quantise_both(c - 1)
                multiply(c - 1)
            if c + 1 < CHUNKS:
                add_hops(c + 1)
            if c >= 2:
                gather_statistics(c - 2)
        quantise(CHUNKS - 1, SELF)

        quantise(CHUNKS - 1, NEIGH)
        multiply(CHUNKS - 1)
        work_up_scalar_statistics()
        gather_statistics(CHUNKS - 2)
        gather_statistics(CHUNKS - 1)

        mean_var = keep.tile([P, 2], F32)
        nc.vector.bn_aggr(out=mean_var[:], in_=stats[:])
        inv_std = keep.tile([P, 1], F32)
        nc.scalar.activation(out=inv_std[:], in_=mean_var[:, 1:2], func=ACT.Abs_reciprocal_sqrt, bias=BN_EPS, scale=1.0)
        nc.vector.scalar_tensor_tensor(
            out=gb_cols[:, 1:2], in0=mean_var[:, 0:1], scalar=-1.0, in1=gb_cols[:, 0:1], op0=ALU.mult, op1=ALU.mult
        )
        slope_shift = keep.tile([P, 2], F32)
        nc.vector.scalar_tensor_tensor(
            out=slope_shift[:], in0=gb_cols[:, 0:2], scalar=inv_std[:, 0:1], in1=gb_cols[:, 2:4], op0=ALU.mult, op1=ALU.add
        )
        slope = slope_shift[:, 0:1]
        shift = slope_shift[:, 1:2]

        out_rows = keep.tile([P, LAYERS, OUT_COLS], F32)
        for c in range(CHUNKS):
            z = out_pool.tile([P, CHUNK_ITEMS], F32)
            nc.vector.tensor_scalar(
                out=z[:], in0=y_of[c], scalar1=slope, scalar2=shift, op0=ALU.mult, op1=ALU.add
            )
            z_bank = bank_pool.tile([P, CHUNK_LAYERS, OUT_COLS], F32, tag="bank")
            for a in range(CHUNK_LAYERS):
                nc.tensor.transpose(z_bank[:, a, :], z[:, a * P : (a + 1) * P], ident[:])
            layers = slice(c * CHUNK_LAYERS, (c + 1) * CHUNK_LAYERS)
            nc.scalar.activation(out=out_rows[:, layers, :], in_=z_bank[:], func=ACT.Sigmoid)
            nc.sync.dma_start(out=out_by_partition[:, layers, :], in_=out_rows[:, layers, :])
